import numpy as np
import ml_dtypes


def mxq(x, axis, fmt="e4m3"):
    dtype, down = {"e4m3": (ml_dtypes.float8_e4m3fn, 7), "e5m2": (ml_dtypes.float8_e5m2, 14)}[fmt]
    v = np.moveaxis(np.asarray(x, np.float32).astype(ml_dtypes.bfloat16).astype(np.float64), axis, -1)
    blocks = v.reshape(v.shape[:-1] + (-1, 32))
    amax = np.abs(blocks).max(-1, keepdims=True)
    byte = np.maximum(np.where(amax > 0, np.frexp(amax)[1] - 1 + 127, 0) - down, 1)
    scale = np.exp2(byte - 127.0)
    codes = (blocks / scale).astype(np.float32).astype(dtype).astype(np.float64)
    return np.moveaxis((codes * scale).reshape(v.shape), -1, axis)


WIDE = False


def mx_kscale(k):
    if not WIDE:
        return np.ones(k)
    levels = np.array([10, -10, 5, -5, 0])
    if k % 512:
        return np.exp2(np.random.permutation(np.resize(levels, k // 32))).repeat(32)
    a = np.empty((k // 512, 16))
    for p in range(k // 512):
        a[p, :8] = np.random.permutation(np.resize(levels, 8))
        for g in range(8):
            far = levels[np.abs(levels - a[p, g]) >= 10]
            a[p, g + 8] = far[np.random.randint(len(far))]
    return np.exp2(a.ravel()).repeat(32)


BF16 = ml_dtypes.bfloat16


def bf(x):
    return np.asarray(x, np.float32).astype(BF16)


def f64(x):
    return np.asarray(x).astype(np.float64)


B, C, D, O = 8, 256, 4096, 256
S0 = 1
S = 2
P = D // (S * (S0 + 1))
K = S * C


def setup_inputs():
    s = mx_kscale(K).reshape(S, C)
    sx = np.tile(np.repeat(s.T, S0 + 1, axis=1), (1, P))
    return {"x": bf(np.random.standard_normal((B, C, D)) * sx),
            "weight": bf(np.random.standard_normal((O, C, 1, S)) / C ** 0.25 / s.T[None, :, None, :])}


def reference(x, weight):
    xp = f64(x).reshape(B, C, D // (S0 + 1), S0 + 1).sum(axis=-1)
    xr = xp.reshape(B, C, P, S)
    a = xr.transpose(0, 2, 3, 1).reshape(B, P, K)
    w = f64(weight)[:, :, 0, :].transpose(2, 1, 0).reshape(K, O)
    out = (mxq(a, 2, "e4m3") @ mxq(w, 0, "e4m3")) / np.sqrt(C)
    return out.transpose(0, 2, 1)

@@ -1,0 +1,145 @@
+from contextlib import ExitStack
+
+import concourse.mybir as mybir
+from concourse.masks import make_identity
+
+BF16 = mybir.dt.bfloat16
+F32 = mybir.dt.float32
+U32 = mybir.dt.uint32
+U8 = mybir.dt.uint8
+FP8X4 = mybir.dt.float8_e4m3fn_x4
+ADD = mybir.AluOpType.add
+COPY = mybir.ActivationFunctionType.Copy
+
+B, C, D, O = 8, 256, 4096, 256
+POS = D // 4
+P = 128
+E = 4
+FLOPS = 2 * B * POS * (2 * C) * O
+
+LOADS = {0: [256, 256, 512], 1: [512, 512], 2: [512, 512], 3: [1024]}
+CHUNKS = {0: [256, 256, 512], 1: [512, 512], 2: [512, 512], 3: [512, 256, 256]}
+QW_AFTER = 1
+
+
+def tile_nonoverlappingconv1d_shared_t_kernel(tc, x, weight, out):
+    nc = tc.nc
+    with ExitStack() as ctx:
+        const = ctx.enter_context(tc.tile_pool(name="const", bufs=1))
+        xpool = ctx.enter_context(tc.tile_pool(name="xpool", bufs=1))
+        opool = ctx.enter_context(tc.tile_pool(name="opool", bufs=1))
+        gpool = ctx.enter_context(tc.tile_pool(name="gpool", bufs=3))
+        qpool = ctx.enter_context(tc.tile_pool(name="qpool", bufs=2))
+        psum = ctx.enter_context(tc.psum_pool(name="psum", bufs=8))
+        ctx.enter_context(tc.manual_schedule())
+
+        w_pad = opool.tile([P, 2, 3 * C], F32, name="late6", align_bytes=64)
+        nc.vector.memset(w_pad[:, :, 0:C], 0.0)
+        nc.vector.memset(w_pad[:, :, 2 * C : 3 * C], 0.0)
+
+        chunks = []
+        n_loads = 0
+        for j in range(B // 2):
+            xb = x[2 * j : 2 * j + 2].rearrange("h (g e) d -> (h g) e d", e=E)
+            tiles = []
+            start = 0
+            for npos in LOADS[j]:
+                xt = xpool.tile([P, E, 4 * npos], BF16, name="xt%d_%d" % (j, start))
+                nc.sync.dma_start(out=xt[:], in_=xb[:, :, 4 * start : 4 * (start + npos)])
+                tiles.append((xt, start, npos))
+                start += npos
+                n_loads += 1
+                if n_loads == 1:
+                    nc.sync.dma_start(
+                        out=w_pad[:, :, C : 2 * C].bitcast(BF16),
+                        in_=weight.rearrange("(q m) c u k -> q m (c u k)", m=2),
+                    )
+            start = 0
+            for npos in CHUNKS[j]:
+                for xt, t0, tn in tiles:
+                    if t0 <= start and start + npos <= t0 + tn:
+                        chunks.append((xt, start - t0, j, start, npos))
+                start += npos
+        n_chunks = len(chunks)
+
+        ident = const.tile([P, P], F32, name="ident")
+        make_identity(nc, ident[:])
+        wg = opool.tile([P, 4 * 2 * P * E], BF16, name="late7", align_bytes=64)
+        for m in range(2):
+            for h in range(2):
+                wt = psum.tile([P, E, P], F32, name="ps")
+                window = w_pad[:, m, (1 - h) * C : (1 - h) * C + 2 * C].rearrange("q (g e) -> q e g", e=E)
+                for e in range(E):
+                    nc.tensor.transpose(out=wt[:, e, :], in_=window[:, e, :], identity=ident[:])
+                i = 2 * m + h
+                nc.scalar.copy(
+                    out=wg[:, i * 2 * P * E : (i + 1) * 2 * P * E].rearrange("p (k q e) -> p k q e", k=2, e=E),
+                    in_=wt[:].rearrange("p e q -> p (e q)").bitcast(BF16).rearrange("p (e q k) -> p k q e", e=E, k=2),
+                )
+        w_codes = const.tile([P, 4 * 2 * P], U32, name="w_codes", align_bytes=64)
+        w_scales = const.tile([P, 4 * 2 * P], U8, name="w_scales", align_bytes=64)
+
+        grouped = {}
+        quantised = {}
+        out_tiles = {}
+
+        def pair_sum(i):
+            xt, n0, j, nb, npos = chunks[i]
+            g = gpool.tile([P, 2 * npos * E], BF16, name="g", align_bytes=64)
+            grouped[i] = g
+            xv = xt[:, :, 4 * n0 : 4 * (n0 + npos)].rearrange("p e (a i k s) -> p a e i k s", i=2, k=2, s=2)
+            for k in range(2):
+                nc.vector.tensor_tensor(
+                    out=g[:, k * npos * E : (k + 1) * npos * E].rearrange("p (a i e) -> p a e i", i=2, e=E),
+                    in0=xv[:, :, :, :, k, 0],
+                    in1=xv[:, :, :, :, k, 1],
+                    op=ADD,
+                )
+
+        def quantise(i):
+            npos = chunks[i][4]
+            codes = qpool.tile([P, 2 * npos], U32, name="codes", align_bytes=64)
+            scales = qpool.tile([P, 2 * npos], U8, name="scales", align_bytes=64)
+            nc.vector.quantize_mx(out=codes[:].bitcast(FP8X4), scales=scales[:], in_=grouped[i][:])
+            quantised[i] = (codes, scales)
+
+        def multiply(i):
+            xt, n0, j, nb, npos = chunks[i]
+            codes, scales = quantised[i]
+            for h in range(2):
+                b = 2 * j + h
+                if nb == 0:
+                    out_tiles[b] = opool.tile([P, 2, POS], F32, name="late%d" % b if b >= 6 else "osb%d" % b, align_bytes=64)
+                osb = out_tiles[b]
+                for m in range(2):
+                    ps = psum.tile([P, 512], F32, name="ps")
+                    for k in range(2):
+                        w_cols = slice((4 * m + 2 * h + k) * P, (4 * m + 2 * h + k + 1) * P)
+                        x_cols = slice(k * npos, (k + 1) * npos)
+                        nc.tensor.matmul_mx(
+                            out=ps[:, :npos],
+                            lhsT=w_codes[:, w_cols].bitcast(FP8X4),
+                            lhsT_scale=w_scales[:, w_cols],
+                            rhs=codes[:, x_cols].bitcast(FP8X4),
+                            rhs_scale=scales[:, x_cols],
+                            start=(k == 0),
+                            stop=(k == 1),
+                        )
+                    if i == n_chunks - 1 and m == 1:
+                        nc.vector.tensor_scalar_mul(osb[:, m, nb : nb + npos], ps[:, :npos], 1.0 / 16.0)
+                    else:
+                        nc.scalar.activation(out=osb[:, m, nb : nb + npos], in_=ps[:, :npos], func=COPY, scale=1.0 / 16.0)
+                ob = out[b].rearrange("(q m) n -> q m n", m=2)
+                if j == B // 2 - 1:
+                    nc.sync.dma_start(out=ob[:, :, nb : nb + npos], in_=osb[:, :, nb : nb + npos])
+                elif nb + npos == POS:
+                    nc.sync.dma_start(out=ob, in_=osb[:])
+
+        for i in range(n_chunks + 1):
+            if i < n_chunks:
+                pair_sum(i)
+            if i == QW_AFTER:
+                nc.vector.quantize_mx(out=w_codes[:].bitcast(FP8X4), scales=w_scales[:], in_=wg[:])
+            if i >= 1:
+                quantise(i - 1)
+                multiply(i - 1)

@@ -87,14 +87,13 @@ def tile_nonoverlappingconv1d_shared_t_kernel(tc, x, weight, out):
             xt, n0, j, nb, npos = chunks[i]
             g = gpool.tile([P, 2 * npos * E], BF16, name="g", align_bytes=64)
             grouped[i] = g
-            xv = xt[:, :, 4 * n0 : 4 * (n0 + npos)].rearrange("p e (a i k s) -> p a e i k s", i=2, k=2, s=2)
-            for k in range(2):
-                nc.vector.tensor_tensor(
-                    out=g[:, k * npos * E : (k + 1) * npos * E].rearrange("p (a i e) -> p a e i", i=2, e=E),
-                    in0=xv[:, :, :, :, k, 0],
-                    in1=xv[:, :, :, :, k, 1],
-                    op=ADD,
-                )
+            xv = xt[:, :, 4 * n0 : 4 * (n0 + npos)].rearrange("p e (n k s) -> p n e k s", k=2, s=2)
+            nc.vector.tensor_tensor(
+                out=g[:].rearrange("p (k n e) -> p n e k", k=2, e=E),
+                in0=xv[:, :, :, :, 0],
+                in1=xv[:, :, :, :, 1],
+                op=ADD,
+            )
 
         def quantise(i):
             npos = chunks[i][4]

@@ -17,9 +17,15 @@ P = 128
 E = 4
 FLOPS = 2 * B * POS * (2 * C) * O
 
-LOADS = {0: [256, 256, 512], 1: [512, 512], 2: [512, 512], 3: [1024]}
-CHUNKS = {0: [256, 256, 512], 1: [512, 512], 2: [512, 512], 3: [512, 256, 256]}
-QW_AFTER = 1
+LOADS = {0: [256, 256, 256, 256], 1: [512, 512], 2: [512, 512], 3: [1024]}
+CHUNKS = {
+    0: [(0, 256, "V"), (256, 256, "V"), (512, 256, "V"), (768, 256, "V")],
+    1: [(0, 512, "V"), (512, 512, "V")],
+    2: [(0, 512, "V"), (512, 512, "V")],
+    3: [(384, 256, "V"), (0, 256, "T"), (640, 256, "V"), (256, 128, "T"), (896, 128, "V")],
+}
+T_AFTER = {6: [0, 1, 2, 3], 7: [4, 5]}
+QW_AFTER = 2
 
 
 def tile_nonoverlappingconv1d_shared_t_kernel(tc, x, weight, out):
@@ -29,7 +35,7 @@ def tile_nonoverlappingconv1d_shared_t_kernel(tc, x, weight, out):
         xpool = ctx.enter_context(tc.tile_pool(name="xpool", bufs=1))
         opool = ctx.enter_context(tc.tile_pool(name="opool", bufs=1))
         gpool = ctx.enter_context(tc.tile_pool(name="gpool", bufs=3))
-        qpool = ctx.enter_context(tc.tile_pool(name="qpool", bufs=2))
+        qpool = ctx.enter_context(tc.tile_pool(name="qpool", bufs=3))
         psum = ctx.enter_context(tc.psum_pool(name="psum", bufs=8))
         ctx.enter_context(tc.manual_schedule())
 
@@ -44,7 +50,7 @@ def tile_nonoverlappingconv1d_shared_t_kernel(tc, x, weight, out):
             tiles = []
             start = 0
             for npos in LOADS[j]:
-                xt = xpool.tile([P, E, 4 * npos], BF16, name="xt%d_%d" % (j, start))
+                xt = xpool.tile([P, E, 4 * npos], BF16, name="xt%d_%d" % (j, start), align_bytes=64)
                 nc.sync.dma_start(out=xt[:], in_=xb[:, :, 4 * start : 4 * (start + npos)])
                 tiles.append((xt, start, npos))
                 start += npos
@@ -54,12 +60,10 @@ def tile_nonoverlappingconv1d_shared_t_kernel(tc, x, weight, out):
                         out=w_pad[:, :, C : 2 * C].bitcast(BF16),
                         in_=weight.rearrange("(q m) c u k -> q m (c u k)", m=2),
                     )
-            start = 0
-            for npos in CHUNKS[j]:
+            for start, npos, by in CHUNKS[j]:
                 for xt, t0, tn in tiles:
                     if t0 <= start and start + npos <= t0 + tn:
-                        chunks.append((xt, start - t0, j, start, npos))
-                start += npos
+                        chunks.append((xt, start - t0, j, start, npos, by))
         n_chunks = len(chunks)
 
         ident = const.tile([P, P], F32, name="ident")
@@ -79,12 +83,19 @@ def tile_nonoverlappingconv1d_shared_t_kernel(tc, x, weight, out):
         w_codes = const.tile([P, 4 * 2 * P], U32, name="w_codes", align_bytes=64)
         w_scales = const.tile([P, 4 * 2 * P], U8, name="w_scales", align_bytes=64)
 
+        ident_b = const.tile([P, P], BF16, name="ident_b")
+        make_identity(nc, ident_b[:])
+        t_chunks = [i for i in range(n_chunks) if chunks[i][5] == "T"]
+        t_groups = [(i, n) for i in t_chunks for n in range(0, chunks[i][4], 64)]
+
         grouped = {}
         quantised = {}
         out_tiles = {}
 
         def pair_sum(i):
-            xt, n0, j, nb, npos = chunks[i]
+            xt, n0, j, nb, npos, by = chunks[i]
+            if by == "T":
+                return
             g = gpool.tile([P, 2 * npos * E], BF16, name="g", align_bytes=64)
             grouped[i] = g
             xv = xt[:, :, 4 * n0 : 4 * (n0 + npos)].rearrange("p e (n k s) -> p n e k s", k=2, s=2)
@@ -95,6 +106,22 @@ def tile_nonoverlappingconv1d_shared_t_kernel(tc, x, weight, out):
                 op=ADD,
             )
 
+        def tensor_pair_sum(i, n):
+            xt, n0, j, nb, npos, by = chunks[i]
+            if n == 0:
+                grouped[i] = xpool.tile([P, 2 * npos * E], BF16, name="xt0_0" if npos == 256 else "xt0_256", align_bytes=64)
+            words = xt[:, :, 4 * (n0 + n) : 4 * (n0 + n + 64)].rearrange("p e (w s) -> p e w s", s=2)
+            ps = psum.tile([P, E, 128], F32, name="ps")
+            for e in range(E):
+                for half in range(2):
+                    nc.tensor.matmul(
+                        out=ps[:, e, :], lhsT=ident_b[:], rhs=words[:, e, :, half], start=(half == 0), stop=(half == 1)
+                    )
+            nc.scalar.copy(
+                out=grouped[i][:].rearrange("p (k n e) -> p k n e", k=2, e=E)[:, :, n : n + 64, :],
+                in_=ps[:].rearrange("p e (n k) -> p k n e", k=2),
+            )
+
         def quantise(i):
             npos = chunks[i][4]
             codes = qpool.tile([P, 2 * npos], U32, name="codes", align_bytes=64)
@@ -103,11 +130,11 @@ def tile_nonoverlappingconv1d_shared_t_kernel(tc, x, weight, out):
             quantised[i] = (codes, scales)
 
         def multiply(i):
-            xt, n0, j, nb, npos = chunks[i]
+            xt, n0, j, nb, npos, by = chunks[i]
             codes, scales = quantised[i]
             for h in range(2):
                 b = 2 * j + h
-                if nb == 0:
+                if b not in out_tiles:
                     out_tiles[b] = opool.tile([P, 2, POS], F32, name="late%d" % b if b >= 6 else "osb%d" % b, align_bytes=64)
                 osb = out_tiles[b]
                 for m in range(2):
@@ -129,16 +156,19 @@ def tile_nonoverlappingconv1d_shared_t_kernel(tc, x, weight, out):
                     else:
                         nc.scalar.activation(out=osb[:, m, nb : nb + npos], in_=ps[:, :npos], func=COPY, scale=1.0 / 16.0)
                 ob = out[b].rearrange("(q m) n -> q m n", m=2)
-                if j == B // 2 - 1:
+                if j >= B // 2 - 2:
                     nc.sync.dma_start(out=ob[:, :, nb : nb + npos], in_=osb[:, :, nb : nb + npos])
                 elif nb + npos == POS:
                     nc.sync.dma_start(out=ob, in_=osb[:])
 
-        for i in range(n_chunks + 1):
+        for i in range(n_chunks + 2):
             if i < n_chunks:
                 pair_sum(i)
             if i == QW_AFTER:
                 nc.vector.quantize_mx(out=w_codes[:].bitcast(FP8X4), scales=w_scales[:], in_=wg[:])
-            if i >= 1:
+            if 1 <= i <= n_chunks:
                 quantise(i - 1)
-                multiply(i - 1)
+            if i >= 2:
+                multiply(i - 2)
+                for group in T_AFTER.get(i - 2, []):
+                    tensor_pair_sum(*t_groups[group])

@@ -24,6 +24,8 @@ CHUNKS = {
     2: [(0, 512, "V"), (512, 512, "V")],
     3: [(384, 256, "V"), (0, 256, "T"), (640, 256, "V"), (256, 128, "T"), (896, 128, "V")],
 }
+OUT_PLACE = {2: ("x", "xt0_0"), 3: ("x", "xt0_256"), 4: ("x", "xt1_0"), 5: ("x", "xt1_512"), 6: ("o", "late6"), 7: ("o", "late7")}
+STAGED = {256: 64, 512: 128}
 T_AFTER = {6: [0, 1, 2, 3], 7: [4, 5]}
 QW_AFTER = 2
 
@@ -34,6 +36,7 @@ def tile_nonoverlappingconv1d_shared_t_kernel(tc, x, weight, out):
         const = ctx.enter_context(tc.tile_pool(name="const", bufs=1))
         xpool = ctx.enter_context(tc.tile_pool(name="xpool", bufs=1))
         opool = ctx.enter_context(tc.tile_pool(name="opool", bufs=1))
+        spool = ctx.enter_context(tc.tile_pool(name="spool", bufs=3))
         gpool = ctx.enter_context(tc.tile_pool(name="gpool", bufs=3))
         qpool = ctx.enter_context(tc.tile_pool(name="qpool", bufs=3))
         psum = ctx.enter_context(tc.psum_pool(name="psum", bufs=8))
@@ -92,24 +95,45 @@ def tile_nonoverlappingconv1d_shared_t_kernel(tc, x, weight, out):
         quantised = {}
         out_tiles = {}
 
+        staged = {}
+
+        def stage(i):
+            xt, n0, j, nb, npos, by = chunks[i]
+            count = STAGED.get(npos, 0) if by == "V" and 2 <= i < 8 else 0
+            if count == 0:
+                return
+            xi = spool.tile([P, 2 * 2 * count * E], BF16, name="xi", align_bytes=64)
+            nc.scalar.copy(
+                out=xi[:].rearrange("p (q n e) -> p n e q", q=4, e=E),
+                in_=xt[:, :, 4 * n0 : 4 * (n0 + count)].rearrange("p e (n q) -> p n e q", q=4),
+            )
+            staged[i] = (xi, count)
+
         def pair_sum(i):
             xt, n0, j, nb, npos, by = chunks[i]
             if by == "T":
                 return
             g = gpool.tile([P, 2 * npos * E], BF16, name="g", align_bytes=64)
             grouped[i] = g
-            xv = xt[:, :, 4 * n0 : 4 * (n0 + npos)].rearrange("p e (n k s) -> p n e k s", k=2, s=2)
+            count = staged[i][1] if i in staged else 0
+            gv = g[:].rearrange("p (k n e) -> p k n e", k=2, e=E)
+            xv = xt[:, :, 4 * (n0 + count) : 4 * (n0 + npos)].rearrange("p e (n k s) -> p n e k s", k=2, s=2)
             nc.vector.tensor_tensor(
-                out=g[:].rearrange("p (k n e) -> p n e k", k=2, e=E),
+                out=gv[:, :, count:, :].rearrange("p k n e -> p n e k"),
                 in0=xv[:, :, :, :, 0],
                 in1=xv[:, :, :, :, 1],
                 op=ADD,
             )
+            if count:
+                pairs = staged[i][0][:].rearrange("p (k s n e) -> p k s n e", k=2, s=2, e=E)
+                nc.vector.tensor_tensor(
+                    out=gv[:, :, :count, :], in0=pairs[:, :, 0], in1=pairs[:, :, 1], op=ADD
+                )
 
         def tensor_pair_sum(i, n):
             xt, n0, j, nb, npos, by = chunks[i]
             if n == 0:
-                grouped[i] = xpool.tile([P, 2 * npos * E], BF16, name="xt0_0" if npos == 256 else "xt0_256", align_bytes=64)
+                grouped[i] = xpool.tile([P, 2 * npos * E], BF16, name="xt0_512" if npos == 256 else "xt0_768", align_bytes=64)
             words = xt[:, :, 4 * (n0 + n) : 4 * (n0 + n + 64)].rearrange("p e (w s) -> p e w s", s=2)
             ps = psum.tile([P, E, 128], F32, name="ps")
             for e in range(E):
@@ -135,7 +159,8 @@ def tile_nonoverlappingconv1d_shared_t_kernel(tc, x, weight, out):
             for h in range(2):
                 b = 2 * j + h
                 if b not in out_tiles:
-                    out_tiles[b] = opool.tile([P, 2, POS], F32, name="late%d" % b if b >= 6 else "osb%d" % b, align_bytes=64)
+                    pool, name = OUT_PLACE.get(b, ("o", "osb%d" % b))
+                    out_tiles[b] = (xpool if pool == "x" else opool).tile([P, 2, POS], F32, name=name, align_bytes=64)
                 osb = out_tiles[b]
                 for m in range(2):
                     ps = psum.tile([P, 512], F32, name="ps")
@@ -162,6 +187,8 @@ def tile_nonoverlappingconv1d_shared_t_kernel(tc, x, weight, out):
                     nc.sync.dma_start(out=ob, in_=osb[:])
 
         for i in range(n_chunks + 2):
+            if i + 1 < n_chunks:
+                stage(i + 1)
             if i < n_chunks:
                 pair_sum(i)
             if i == QW_AFTER:

@@ -17,17 +17,18 @@ P = 128
 E = 4
 FLOPS = 2 * B * POS * (2 * C) * O
 
-LOADS = {0: [256, 256, 256, 256], 1: [512, 512], 2: [512, 512], 3: [1024]}
+LOADS = {0: [256, 256, 512], 1: [512, 512], 2: [512, 512], 3: [1024]}
 CHUNKS = {
-    0: [(0, 256, "V"), (256, 256, "V"), (512, 256, "V"), (768, 256, "V")],
+    0: [(0, 256, "V"), (256, 256, "V"), (512, 512, "V")],
     1: [(0, 512, "V"), (512, 512, "V")],
     2: [(0, 512, "V"), (512, 512, "V")],
-    3: [(384, 256, "V"), (0, 256, "T"), (640, 256, "V"), (256, 128, "T"), (896, 128, "V")],
+    3: [(0, 256, "V"), (256, 256, "T"), (512, 256, "V"), (768, 128, "T"), (896, 128, "V")],
 }
-OUT_PLACE = {2: ("x", "xt0_0"), 3: ("x", "xt0_256"), 4: ("x", "xt1_0"), 5: ("x", "xt1_512"), 6: ("o", "late6"), 7: ("o", "late7")}
+STORES = {3: [(0, 768), (768, 256)]}
+OUT_PLACE = {2: ("x", "xt0_0"), 3: ("x", "xt0_512"), 4: ("x", "xt1_0"), 5: ("x", "xt1_512"), 6: ("o", "late6"), 7: ("o", "late7")}
 STAGED = {256: 64, 512: 128}
-T_AFTER = {6: [0, 1, 2, 3], 7: [4, 5]}
-QW_AFTER = 2
+T_AFTER = {5: [0, 1, 2, 3], 6: [4, 5]}
+QW_AFTER = 1
 
 
 def tile_nonoverlappingconv1d_shared_t_kernel(tc, x, weight, out):
@@ -99,7 +100,7 @@ def tile_nonoverlappingconv1d_shared_t_kernel(tc, x, weight, out):
 
         def stage(i):
             xt, n0, j, nb, npos, by = chunks[i]
-            count = STAGED.get(npos, 0) if by == "V" and 2 <= i < 8 else 0
+            count = STAGED.get(npos, 0) if by == "V" and 2 <= i < 7 else 0
             if count == 0:
                 return
             xi = spool.tile([P, 2 * 2 * count * E], BF16, name="xi", align_bytes=64)
@@ -133,7 +134,7 @@ def tile_nonoverlappingconv1d_shared_t_kernel(tc, x, weight, out):
         def tensor_pair_sum(i, n):
             xt, n0, j, nb, npos, by = chunks[i]
             if n == 0:
-                grouped[i] = xpool.tile([P, 2 * npos * E], BF16, name="xt0_512" if npos == 256 else "xt0_768", align_bytes=64)
+                grouped[i] = const.tile([P, 2 * npos * E], BF16, name="g_t%d" % i, align_bytes=64)
             words = xt[:, :, 4 * (n0 + n) : 4 * (n0 + n + 64)].rearrange("p e (w s) -> p e w s", s=2)
             ps = psum.tile([P, E, 128], F32, name="ps")
             for e in range(E):
@@ -180,22 +181,24 @@ def tile_nonoverlappingconv1d_shared_t_kernel(tc, x, weight, out):
                         nc.vector.tensor_scalar_mul(osb[:, m, nb : nb + npos], ps[:, :npos], 1.0 / 16.0)
                     else:
                         nc.scalar.activation(out=osb[:, m, nb : nb + npos], in_=ps[:, :npos], func=COPY, scale=1.0 / 16.0)
-                ob = out[b].rearrange("(q m) n -> q m n", m=2)
-                if j >= B // 2 - 2:
-                    nc.sync.dma_start(out=ob[:, :, nb : nb + npos], in_=osb[:, :, nb : nb + npos])
-                elif nb + npos == POS:
-                    nc.sync.dma_start(out=ob, in_=osb[:])
+            for s0, sn in STORES.get(j, [(0, POS)]):
+                if nb + npos == s0 + sn:
+                    for h in range(2):
+                        nc.sync.dma_start(
+                            out=out[2 * j + h].rearrange("(q m) n -> q m n", m=2)[:, :, s0 : s0 + sn],
+                            in_=out_tiles[2 * j + h][:, :, s0 : s0 + sn],
+                        )
 
         for i in range(n_chunks + 2):
-            if i + 1 < n_chunks:
-                stage(i + 1)
             if i < n_chunks:
                 pair_sum(i)
-            if i == QW_AFTER:
-                nc.vector.quantize_mx(out=w_codes[:].bitcast(FP8X4), scales=w_scales[:], in_=wg[:])
             if 1 <= i <= n_chunks:
                 quantise(i - 1)
+            if i == QW_AFTER:
+                nc.vector.quantize_mx(out=w_codes[:].bitcast(FP8X4), scales=w_scales[:], in_=wg[:])
             if i >= 2:
                 multiply(i - 2)
                 for group in T_AFTER.get(i - 2, []):
                     tensor_pair_sum(*t_groups[group])
+            if i + 1 < n_chunks:
+                stage(i + 1)

@@ -17,17 +17,17 @@ P = 128
 E = 4
 FLOPS = 2 * B * POS * (2 * C) * O
 
-LOADS = {0: [256, 256, 512], 1: [512, 512], 2: [512, 512], 3: [1024]}
+LOADS = {0: [384, 640], 1: [512, 512], 2: [512, 512], 3: [1024]}
 CHUNKS = {
-    0: [(0, 256, "V"), (256, 256, "V"), (512, 512, "V")],
+    0: [(0, 256, "V"), (256, 128, "V"), (384, 128, "T"), (512, 512, "V")],
     1: [(0, 512, "V"), (512, 512, "V")],
     2: [(0, 512, "V"), (512, 512, "V")],
-    3: [(0, 256, "V"), (256, 256, "T"), (512, 256, "V"), (768, 128, "T"), (896, 128, "V")],
+    3: [(0, 256, "V"), (256, 256, "T"), (512, 256, "V"), (768, 128, "V"), (896, 128, "V")],
 }
 STORES = {3: [(0, 768), (768, 256)]}
-OUT_PLACE = {2: ("x", "xt0_0"), 3: ("x", "xt0_512"), 4: ("x", "xt1_0"), 5: ("x", "xt1_512"), 6: ("o", "late6"), 7: ("o", "late7")}
+OUT_PLACE = {2: ("x", "xt0_0"), 3: ("x", "xt0_384"), 4: ("x", "xt1_0"), 5: ("x", "xt1_512"), 6: ("o", "late6"), 7: ("o", "late7")}
 STAGED = {256: 64, 512: 128}
-T_AFTER = {5: [0, 1, 2, 3], 6: [4, 5]}
+T_AT = {1: [0, 1], 8: [2, 3, 4, 5]}
 QW_AFTER = 1
 
 
@@ -43,12 +43,14 @@ def tile_nonoverlappingconv1d_shared_t_kernel(tc, x, weight, out):
         psum = ctx.enter_context(tc.psum_pool(name="psum", bufs=8))
         ctx.enter_context(tc.manual_schedule())
 
-        w_pad = opool.tile([P, 2, 3 * C], F32, name="late6", align_bytes=64)
-        nc.vector.memset(w_pad[:, :, 0:C], 0.0)
-        nc.vector.memset(w_pad[:, :, 2 * C : 3 * C], 0.0)
+        w_pad = opool.tile([P, 5 * C], F32, name="late6", align_bytes=64)
+        for z in range(3):
+            nc.vector.memset(w_pad[:, 2 * z * C : (2 * z + 1) * C], 0.0)
 
+        w_rows = weight.rearrange("(q m) c u k -> m q (c u k)", m=2)
+        for m in range(2):
+            nc.sync.dma_start(out=w_pad[:, (2 * m + 1) * C : (2 * m + 2) * C].bitcast(BF16), in_=w_rows[m])
         chunks = []
-        n_loads = 0
         for j in range(B // 2):
             xb = x[2 * j : 2 * j + 2].rearrange("h (g e) d -> (h g) e d", e=E)
             tiles = []
@@ -58,12 +60,6 @@ def tile_nonoverlappingconv1d_shared_t_kernel(tc, x, weight, out):
                 nc.sync.dma_start(out=xt[:], in_=xb[:, :, 4 * start : 4 * (start + npos)])
                 tiles.append((xt, start, npos))
                 start += npos
-                n_loads += 1
-                if n_loads == 1:
-                    nc.sync.dma_start(
-                        out=w_pad[:, :, C : 2 * C].bitcast(BF16),
-                        in_=weight.rearrange("(q m) c u k -> q m (c u k)", m=2),
-                    )
             for start, npos, by in CHUNKS[j]:
                 for xt, t0, tn in tiles:
                     if t0 <= start and start + npos <= t0 + tn:
@@ -76,11 +72,12 @@ def tile_nonoverlappingconv1d_shared_t_kernel(tc, x, weight, out):
         for m in range(2):
             for h in range(2):
                 wt = psum.tile([P, E, P], F32, name="ps")
-                window = w_pad[:, m, (1 - h) * C : (1 - h) * C + 2 * C].rearrange("q (g e) -> q e g", e=E)
+                window = w_pad[:, (2 * m + 1 - h) * C : (2 * m + 3 - h) * C].rearrange("q (g e) -> q e g", e=E)
                 for e in range(E):
                     nc.tensor.transpose(out=wt[:, e, :], in_=window[:, e, :], identity=ident[:])
                 i = 2 * m + h
-                nc.scalar.copy(
+                copy = nc.vector.tensor_copy if h == 0 else nc.scalar.copy
+                copy(
                     out=wg[:, i * 2 * P * E : (i + 1) * 2 * P * E].rearrange("p (k q e) -> p k q e", k=2, e=E),
                     in_=wt[:].rearrange("p e q -> p (e q)").bitcast(BF16).rearrange("p (e q k) -> p k q e", e=E, k=2),
                 )
@@ -100,7 +97,7 @@ def tile_nonoverlappingconv1d_shared_t_kernel(tc, x, weight, out):
 
         def stage(i):
             xt, n0, j, nb, npos, by = chunks[i]
-            count = STAGED.get(npos, 0) if by == "V" and 2 <= i < 7 else 0
+            count = STAGED.get(npos, 0) if by == "V" and 3 <= i < 8 else 0
             if count == 0:
                 return
             xi = spool.tile([P, 2 * 2 * count * E], BF16, name="xi", align_bytes=64)
@@ -125,11 +122,14 @@ def tile_nonoverlappingconv1d_shared_t_kernel(tc, x, weight, out):
                 in1=xv[:, :, :, :, 1],
                 op=ADD,
             )
-            if count:
-                pairs = staged[i][0][:].rearrange("p (k s n e) -> p k s n e", k=2, s=2, e=E)
-                nc.vector.tensor_tensor(
-                    out=gv[:, :, :count, :], in0=pairs[:, :, 0], in1=pairs[:, :, 1], op=ADD
-                )
+
+        def staged_pair_sum(i):
+            if i not in staged:
+                return
+            xi, count = staged[i]
+            gv = grouped[i][:].rearrange("p (k n e) -> p k n e", k=2, e=E)
+            pairs = xi[:].rearrange("p (k s n e) -> p k s n e", k=2, s=2, e=E)
+            nc.vector.tensor_tensor(out=gv[:, :, :count, :], in0=pairs[:, :, 0], in1=pairs[:, :, 1], op=ADD)
 
         def tensor_pair_sum(i, n):
             xt, n0, j, nb, npos, by = chunks[i]
@@ -196,9 +196,11 @@ def tile_nonoverlappingconv1d_shared_t_kernel(tc, x, weight, out):
                 quantise(i - 1)
             if i == QW_AFTER:
                 nc.vector.quantize_mx(out=w_codes[:].bitcast(FP8X4), scales=w_scales[:], in_=wg[:])
-            if i >= 2:
-                multiply(i - 2)
-                for group in T_AFTER.get(i - 2, []):
-                    tensor_pair_sum(*t_groups[group])
+            if i < n_chunks:
+                staged_pair_sum(i)
             if i + 1 < n_chunks:
                 stage(i + 1)
+            if i >= 2:
+                multiply(i - 2)
+            for group in T_AT.get(i, []):
+                tensor_pair_sum(*t_groups[group])

from contextlib import ExitStack

import concourse.mybir as mybir
from concourse.masks import make_identity

BF16 = mybir.dt.bfloat16
F32 = mybir.dt.float32
U32 = mybir.dt.uint32
U8 = mybir.dt.uint8
FP8X4 = mybir.dt.float8_e4m3fn_x4
ADD = mybir.AluOpType.add
COPY = mybir.ActivationFunctionType.Copy

B, C, D, O = 8, 256, 4096, 256
POS = D // 4
P = 128
E = 4
FLOPS = 2 * B * POS * (2 * C) * O

LOADS = {0: [384, 640], 1: [512, 512], 2: [512, 512], 3: [1024]}
CHUNKS = {
    0: [(0, 256, "V"), (256, 128, "V"), (384, 128, "T"), (512, 512, "V")],
    1: [(0, 512, "V"), (512, 512, "V")],
    2: [(0, 512, "V"), (512, 512, "V")],
    3: [(0, 256, "V"), (256, 256, "T"), (512, 256, "V"), (768, 128, "V"), (896, 128, "V")],
}
STORES = {3: [(0, 768), (768, 256)]}
OUT_PLACE = {2: ("x", "xt0_0"), 3: ("x", "xt0_384"), 4: ("x", "xt1_0"), 5: ("x", "xt1_512"), 6: ("o", "late6"), 7: ("o", "late7")}
STAGED = {256: 64, 512: 128}
T_AT = {1: [0, 1], 8: [2, 3, 4, 5]}
QW_AFTER = 1


def tile_nonoverlappingconv1d_shared_t_kernel(tc, x, weight, out):
    nc = tc.nc
    with ExitStack() as ctx:
        const = ctx.enter_context(tc.tile_pool(name="const", bufs=1))
        xpool = ctx.enter_context(tc.tile_pool(name="xpool", bufs=1))
        opool = ctx.enter_context(tc.tile_pool(name="opool", bufs=1))
        spool = ctx.enter_context(tc.tile_pool(name="spool", bufs=3))
        gpool = ctx.enter_context(tc.tile_pool(name="gpool", bufs=3))
        qpool = ctx.enter_context(tc.tile_pool(name="qpool", bufs=3))
        psum = ctx.enter_context(tc.psum_pool(name="psum", bufs=8))
        ctx.enter_context(tc.manual_schedule())

        w_pad = opool.tile([P, 5 * C], F32, name="late6", align_bytes=64)
        for z in range(3):
            nc.vector.memset(w_pad[:, 2 * z * C : (2 * z + 1) * C], 0.0)

        w_rows = weight.rearrange("(q m) c u k -> m q (c u k)", m=2)
        for m in range(2):
            nc.sync.dma_start(out=w_pad[:, (2 * m + 1) * C : (2 * m + 2) * C].bitcast(BF16), in_=w_rows[m])
        chunks = []
        for j in range(B // 2):
            xb = x[2 * j : 2 * j + 2].rearrange("h (g e) d -> (h g) e d", e=E)
            tiles = []
            start = 0
            for npos in LOADS[j]:
                xt = xpool.tile([P, E, 4 * npos], BF16, name="xt%d_%d" % (j, start), align_bytes=64)
                nc.sync.dma_start(out=xt[:], in_=xb[:, :, 4 * start : 4 * (start + npos)])
                tiles.append((xt, start, npos))
                start += npos
            for start, npos, by in CHUNKS[j]:
                for xt, t0, tn in tiles:
                    if t0 <= start and start + npos <= t0 + tn:
                        chunks.append((xt, start - t0, j, start, npos, by))
        n_chunks = len(chunks)

        ident = const.tile([P, P], F32, name="ident")
        make_identity(nc, ident[:])
        wg = opool.tile([P, 4 * 2 * P * E], BF16, name="late7", align_bytes=64)
        for m in range(2):
            for h in range(2):
                wt = psum.tile([P, E, P], F32, name="ps")
                window = w_pad[:, (2 * m + 1 - h) * C : (2 * m + 3 - h) * C].rearrange("q (g e) -> q e g", e=E)
                for e in range(E):
                    nc.tensor.transpose(out=wt[:, e, :], in_=window[:, e, :], identity=ident[:])
                i = 2 * m + h
                copy = nc.vector.tensor_copy if h == 0 else nc.scalar.copy
                copy(
                    out=wg[:, i * 2 * P * E : (i + 1) * 2 * P * E].rearrange("p (k q e) -> p k q e", k=2, e=E),
                    in_=wt[:].rearrange("p e q -> p (e q)").bitcast(BF16).rearrange("p (e q k) -> p k q e", e=E, k=2),
                )
        w_codes = const.tile([P, 4 * 2 * P], U32, name="w_codes", align_bytes=64)
        w_scales = const.tile([P, 4 * 2 * P], U8, name="w_scales", align_bytes=64)

        ident_b = const.tile([P, P], BF16, name="ident_b")
        make_identity(nc, ident_b[:])
        t_chunks = [i for i in range(n_chunks) if chunks[i][5] == "T"]
        t_groups = [(i, n) for i in t_chunks for n in range(0, chunks[i][4], 64)]

        grouped = {}
        quantised = {}
        out_tiles = {}

        staged = {}

        def stage(i):
            xt, n0, j, nb, npos, by = chunks[i]
            count = STAGED.get(npos, 0) if by == "V" and 3 <= i < 8 else 0
            if count == 0:
                return
            xi = spool.tile([P, 2 * 2 * count * E], BF16, name="xi", align_bytes=64)
            nc.scalar.copy(
                out=xi[:].rearrange("p (q n e) -> p n e q", q=4, e=E),
                in_=xt[:, :, 4 * n0 : 4 * (n0 + count)].rearrange("p e (n q) -> p n e q", q=4),
            )
            staged[i] = (xi, count)

        def pair_sum(i):
            xt, n0, j, nb, npos, by = chunks[i]
            if by == "T":
                return
            g = gpool.tile([P, 2 * npos * E], BF16, name="g", align_bytes=64)
            grouped[i] = g
            count = staged[i][1] if i in staged else 0
            gv = g[:].rearrange("p (k n e) -> p k n e", k=2, e=E)
            xv = xt[:, :, 4 * (n0 + count) : 4 * (n0 + npos)].rearrange("p e (n k s) -> p n e k s", k=2, s=2)
            nc.vector.tensor_tensor(
                out=gv[:, :, count:, :].rearrange("p k n e -> p n e k"),
                in0=xv[:, :, :, :, 0],
                in1=xv[:, :, :, :, 1],
                op=ADD,
            )

        def staged_pair_sum(i):
            if i not in staged:
                return
            xi, count = staged[i]
            gv = grouped[i][:].rearrange("p (k n e) -> p k n e", k=2, e=E)
            pairs = xi[:].rearrange("p (k s n e) -> p k s n e", k=2, s=2, e=E)
            nc.vector.tensor_tensor(out=gv[:, :, :count, :], in0=pairs[:, :, 0], in1=pairs[:, :, 1], op=ADD)

        def tensor_pair_sum(i, n):
            xt, n0, j, nb, npos, by = chunks[i]
            if n == 0:
                grouped[i] = const.tile([P, 2 * npos * E], BF16, name="g_t%d" % i, align_bytes=64)
            words = xt[:, :, 4 * (n0 + n) : 4 * (n0 + n + 64)].rearrange("p e (w s) -> p e w s", s=2)
            ps = psum.tile([P, E, 128], F32, name="ps")
            for e in range(E):
                for half in range(2):
                    nc.tensor.matmul(
                        out=ps[:, e, :], lhsT=ident_b[:], rhs=words[:, e, :, half], start=(half == 0), stop=(half == 1)
                    )
            nc.scalar.copy(
                out=grouped[i][:].rearrange("p (k n e) -> p k n e", k=2, e=E)[:, :, n : n + 64, :],
                in_=ps[:].rearrange("p e (n k) -> p k n e", k=2),
            )

        def quantise(i):
            npos = chunks[i][4]
            codes = qpool.tile([P, 2 * npos], U32, name="codes", align_bytes=64)
            scales = qpool.tile([P, 2 * npos], U8, name="scales", align_bytes=64)
            nc.vector.quantize_mx(out=codes[:].bitcast(FP8X4), scales=scales[:], in_=grouped[i][:])
            quantised[i] = (codes, scales)

        def multiply(i):
            xt, n0, j, nb, npos, by = chunks[i]
            codes, scales = quantised[i]
            for h in range(2):
                b = 2 * j + h
                if b not in out_tiles:
                    pool, name = OUT_PLACE.get(b, ("o", "osb%d" % b))
                    out_tiles[b] = (xpool if pool == "x" else opool).tile([P, 2, POS], F32, name=name, align_bytes=64)
                osb = out_tiles[b]
                for m in range(2):
                    ps = psum.tile([P, 512], F32, name="ps")
                    for k in range(2):
                        w_cols = slice((4 * m + 2 * h + k) * P, (4 * m + 2 * h + k + 1) * P)
                        x_cols = slice(k * npos, (k + 1) * npos)
                        nc.tensor.matmul_mx(
                            out=ps[:, :npos],
                            lhsT=w_codes[:, w_cols].bitcast(FP8X4),
                            lhsT_scale=w_scales[:, w_cols],
                            rhs=codes[:, x_cols].bitcast(FP8X4),
                            rhs_scale=scales[:, x_cols],
                            start=(k == 0),
                            stop=(k == 1),
                        )
                    if i == n_chunks - 1 and m == 1:
                        nc.vector.tensor_scalar_mul(osb[:, m, nb : nb + npos], ps[:, :npos], 1.0 / 16.0)
                    else:
                        nc.scalar.activation(out=osb[:, m, nb : nb + npos], in_=ps[:, :npos], func=COPY, scale=1.0 / 16.0)
            for s0, sn in STORES.get(j, [(0, POS)]):
                if nb + npos == s0 + sn:
                    for h in range(2):
                        nc.sync.dma_start(
                            out=out[2 * j + h].rearrange("(q m) n -> q m n", m=2)[:, :, s0 : s0 + sn],
                            in_=out_tiles[2 * j + h][:, :, s0 : s0 + sn],
                        )

        for i in range(n_chunks + 2):
            if i < n_chunks:
                pair_sum(i)
            if 1 <= i <= n_chunks:
                quantise(i - 1)
            if i == QW_AFTER:
                nc.vector.quantize_mx(out=w_codes[:].bitcast(FP8X4), scales=w_scales[:], in_=wg[:])
            if i < n_chunks:
                staged_pair_sum(i)
            if i + 1 < n_chunks:
                stage(i + 1)
            if i >= 2:
                multiply(i - 2)
            for group in T_AT.get(i, []):
                tensor_pair_sum(*t_groups[group])
